import numpy as np
import ml_dtypes


def mxq(x, axis, fmt="e4m3"):
    dtype, down = {"e4m3": (ml_dtypes.float8_e4m3fn, 7), "e5m2": (ml_dtypes.float8_e5m2, 14)}[fmt]
    v = np.moveaxis(np.asarray(x, np.float32).astype(ml_dtypes.bfloat16).astype(np.float64), axis, -1)
    blocks = v.reshape(v.shape[:-1] + (-1, 32))
    amax = np.abs(blocks).max(-1, keepdims=True)
    byte = np.maximum(np.where(amax > 0, np.frexp(amax)[1] - 1 + 127, 0) - down, 1)
    scale = np.exp2(byte - 127.0)
    codes = (blocks / scale).astype(np.float32).astype(dtype).astype(np.float64)
    return np.moveaxis((codes * scale).reshape(v.shape), -1, axis)


WIDE = False


def mx_kscale(k):
    if not WIDE:
        return np.ones(k)
    levels = np.array([10, -10, 5, -5, 0])
    if k % 512:
        return np.exp2(np.random.permutation(np.resize(levels, k // 32))).repeat(32)
    a = np.empty((k // 512, 16))
    for p in range(k // 512):
        a[p, :8] = np.random.permutation(np.resize(levels, 8))
        for g in range(8):
            far = levels[np.abs(levels - a[p, g]) >= 10]
            a[p, g + 8] = far[np.random.randint(len(far))]
    return np.exp2(a.ravel()).repeat(32)


BF16 = ml_dtypes.bfloat16


def bf(x):
    return np.asarray(x, np.float32).astype(BF16)


def f64(x):
    return np.asarray(x).astype(np.float64)


B, S, D, NH, NKV, HD, QB = 1, 512, 2048, 16, 4, 128, 512
Q_DIM = NH * HD
KV_DIM = NKV * HD


def rot(t, f0, f1):
    tp = t.reshape(t.shape[:-1] + (HD // 2, 2))
    t0, t1 = tp[..., 0], tp[..., 1]
    row1 = t0 * f0 + t1 * f1
    row0 = t0 * f1 - t1 * f0
    return np.stack([row0, row1], axis=-1).reshape(t.shape)


def setup_inputs():
    s = mx_kscale(D)
    return {"x": bf(np.random.standard_normal((B, S, D)) * s),
            "freqs_cis": bf(np.random.standard_normal((S, HD))),
            "Wqkv": bf(np.random.standard_normal((Q_DIM + 2 * KV_DIM, D)) / np.sqrt(D) / s)}


def reference(x, freqs_cis, Wqkv):
    xqkv = mxq(f64(x), 2, "e4m3") @ mxq(f64(Wqkv), 1, "e4m3").T
    xq = xqkv[..., :Q_DIM].reshape(B, S, NH, HD)
    xk = xqkv[..., Q_DIM:Q_DIM + KV_DIM].reshape(B, S, NKV, HD)
    xv = xqkv[..., Q_DIM + KV_DIM:].reshape(B, S, NKV, HD)
    f = f64(freqs_cis).reshape(S, 1, HD // 2, 2)
    f0, f1 = f[..., 0], f[..., 1]
    q_rot = rot(xq, f0, f1).transpose(0, 2, 1, 3)
    k_rot = rot(xk, f0, f1).transpose(0, 2, 1, 3)
    v = xv.transpose(0, 2, 1, 3)
    return q_rot, k_rot, v

@@ -1,0 +1,181 @@
+from contextlib import ExitStack
+
+import concourse.mybir as mybir
+from concourse.masks import make_identity
+
+F32 = mybir.dt.float32
+BF16 = mybir.dt.bfloat16
+U32 = mybir.dt.uint32
+U8 = mybir.dt.uint8
+FP8X4 = mybir.dt.float8_e4m3fn_x4
+MULT = mybir.AluOpType.mult
+ADD = mybir.AluOpType.add
+
+P = 128
+POSITIONS = 512
+K = 2048
+HEAD = 128
+PAIRS = HEAD // 2
+Q_HEADS, K_HEADS, V_HEADS = 16, 4, 4
+
+K_PASS = 4 * P
+PASSES = K // K_PASS
+WORDS = K_PASS // 2
+
+SLAB = 256
+SLAB_TILES = SLAB // P
+SLAB_HEADS = SLAB // HEAD
+TILES = POSITIONS // P
+X_SLABS = POSITIONS // SLAB
+W_SLABS = (Q_HEADS + K_HEADS + V_HEADS) // SLAB_HEADS
+ROTATED_SLABS = (Q_HEADS + K_HEADS) // SLAB_HEADS
+RAW_SLABS_IN_SBUF = 8
+
+FLOPS = 2 * POSITIONS * K * (Q_HEADS + K_HEADS + V_HEADS) * HEAD
+
+
+def tile_rlaattention_pa_kernel(tc, x, freqs_cis, Wqkv, out_0, out_1, out_2):
+    nc = tc.nc
+
+    x_rows = x.flatten_outer_dims().rearrange("(p i) k -> p i k", i=TILES)
+    freq_rows = freqs_cis.rearrange("(p i) d -> p i d", i=TILES)
+    slab_rows = [
+        out.rearrange("b h (p i) d -> p (b h) i d", i=TILES)[:, h : h + SLAB_HEADS]
+        for out, heads in ((out_0, Q_HEADS), (out_1, K_HEADS), (out_2, V_HEADS))
+        for h in range(0, heads, SLAB_HEADS)
+    ]
+
+    with ExitStack() as ctx:
+        ctx.enter_context(tc.manual_schedule())
+        keep = ctx.enter_context(tc.tile_pool(name="keep", bufs=1))
+        raw_pool = ctx.enter_context(tc.tile_pool(name="raw", bufs=RAW_SLABS_IN_SBUF))
+        stage = ctx.enter_context(tc.tile_pool(name="stage", bufs=2 * PASSES))
+        w_mx = ctx.enter_context(tc.tile_pool(name="w_mx", bufs=3))
+        products = ctx.enter_context(tc.tile_pool(name="products", bufs=4))
+        results = ctx.enter_context(tc.tile_pool(name="results", bufs=10))
+        flipped_banks = ctx.enter_context(tc.psum_pool(name="flipped_banks", bufs=4))
+        sum_banks = ctx.enter_context(tc.psum_pool(name="sum_banks", bufs=4))
+
+        def load_w_slab(s):
+            w_raw = raw_pool.tile([P, SLAB_TILES, K], BF16, tag="w_raw")
+            nc.sync.dma_start(
+                out=w_raw[:],
+                in_=Wqkv[SLAB * s : SLAB * (s + 1), :].rearrange("(r p) k -> p r k", p=P),
+            )
+            return w_raw
+
+        def quantise_slab(raw, codes, scales, vector_helps):
+            for c in range(PASSES):
+                flipped = flipped_banks.tile([P, 2, SLAB], F32, tag="flipped")
+                for u in range(2):
+                    for r in range(SLAB_TILES):
+                        nc.tensor.transpose(
+                            flipped[:, u, P * r : P * (r + 1)],
+                            raw[:, r, :].bitcast(F32)[:, WORDS * c + u : WORDS * (c + 1) : 2],
+                            identity[:],
+                        )
+                grouped = stage.tile([P, 4 * SLAB], BF16, tag="grouped", align_bytes=64)
+                side_by_side = grouped[:].bitcast(F32).rearrange("p (n u) -> p n u", u=2)
+                planes = flipped[:].rearrange("p u n -> p n u")
+                if vector_helps and c == 1:
+                    nc.vector.tensor_copy(out=side_by_side, in_=planes)
+                else:
+                    nc.scalar.copy(out=side_by_side, in_=planes)
+                nc.vector.quantize_mx(
+                    out=codes[:, c, :].bitcast(FP8X4), scales=scales[:, c, :], in_=grouped[:]
+                )
+
+        freq_raw = keep.tile([P, TILES, PAIRS, 2], BF16)
+        nc.scalar.dma_start(
+            out=freq_raw[:].rearrange("p i j e -> p i (j e)"), in_=freq_rows
+        )
+        x_raws = []
+        for s in range(X_SLABS):
+            x_raw = keep.tile([P, SLAB_TILES, K], BF16, name="x_raw%d" % s)
+            nc.sync.dma_start(
+                out=x_raw[:], in_=x_rows[:, SLAB_TILES * s : SLAB_TILES * (s + 1), :]
+            )
+            x_raws.append(x_raw)
+        w_raws = [load_w_slab(s) for s in range(RAW_SLABS_IN_SBUF)]
+
+        identity = keep.tile([P, P], F32)
+        make_identity(nc, identity[:])
+
+        for_even = keep.tile([P, TILES, PAIRS, 2], F32)
+        for_odd = keep.tile([P, TILES, PAIRS, 2], F32)
+        nc.vector.tensor_copy(out=for_even[:, :, :, 0], in_=freq_raw[:, :, :, 1])
+        nc.vector.tensor_copy(out=for_even[:, :, :, 1], in_=freq_raw[:, :, :, 0])
+        nc.vector.tensor_scalar_mul(for_odd[:, :, :, 0], freq_raw[:, :, :, 0], -1.0)
+        nc.vector.tensor_copy(out=for_odd[:, :, :, 1], in_=freq_raw[:, :, :, 1])
+
+        x_codes = keep.tile([P, PASSES, POSITIONS], U32, align_bytes=64)
+        x_scales = keep.tile([P, PASSES, POSITIONS], U8, align_bytes=64)
+        for s in range(X_SLABS):
+            columns = slice(SLAB * s, SLAB * (s + 1))
+            quantise_slab(x_raws[s], x_codes[:, :, columns], x_scales[:, :, columns], True)
+
+        def prepare_w_slab(s):
+            w_codes = w_mx.tile([P, PASSES, SLAB], U32, tag="w_codes", align_bytes=64)
+            w_scales = w_mx.tile([P, PASSES, SLAB], U8, tag="w_scales", align_bytes=64)
+            quantise_slab(w_raws[s], w_codes, w_scales, s <= 1)
+            if s + RAW_SLABS_IN_SBUF < W_SLABS:
+                w_raws.append(load_w_slab(s + RAW_SLABS_IN_SBUF))
+            return w_codes, w_scales
+
+        by_member = [P, 2, SLAB_HEADS, PAIRS, 2]
+        prepared = prepare_w_slab(0)
+        for s in range(W_SLABS):
+            w_codes, w_scales = prepared
+            if s + 1 < W_SLABS:
+                prepared = prepare_w_slab(s + 1)
+
+            for first_tile in range(0, TILES, 2):
+                sums = sum_banks.tile([P, 2, SLAB], F32, tag="sums")
+                for t in range(2):
+                    positions = slice(P * (first_tile + t), P * (first_tile + t + 1))
+                    for c in range(PASSES):
+                        nc.tensor.matmul_mx(
+                            out=sums[:, t, :],
+                            lhsT=x_codes[:, c, positions].bitcast(FP8X4),
+                            lhsT_scale=x_scales[:, c, positions],
+                            rhs=w_codes[:, c, :].bitcast(FP8X4),
+                            rhs_scale=w_scales[:, c, :],
+                            start=(c == 0),
+                            stop=(c == PASSES - 1),
+                        )
+                result = results.tile([P, SLAB_HEADS, 2, HEAD], F32, tag="result")
+                result_by_tile = result[:].rearrange("p h t d -> p t h d")
+                if s < ROTATED_SLABS:
+                    members = sums[:].rearrange(
+                        "p t (h j e) -> p t h j e", h=SLAB_HEADS, e=2
+                    )
+                    tiles = slice(first_tile, first_tile + 2)
+                    from_even = products.tile(by_member, F32, tag="from_even")
+                    from_odd = products.tile(by_member, F32, tag="from_odd")
+                    nc.vector.tensor_tensor(
+                        out=from_even[:],
+                        in0=members[:, :, :, :, 0:1].to_broadcast(by_member),
+                        in1=for_even[:, tiles].unsqueeze(2).to_broadcast(by_member),
+                        op=MULT,
+                    )
+                    nc.vector.tensor_tensor(
+                        out=from_odd[:],
+                        in0=members[:, :, :, :, 1:2].to_broadcast(by_member),
+                        in1=for_odd[:, tiles].unsqueeze(2).to_broadcast(by_member),
+                        op=MULT,
+                    )
+                    nc.gpsimd.tensor_tensor(
+                        out=result_by_tile,
+                        in0=from_even[:].rearrange("p t h j e -> p t h (j e)"),
+                        in1=from_odd[:].rearrange("p t h j e -> p t h (j e)"),
+                        op=ADD,
+                    )
+                else:
+                    sums_by_head = sums[:].rearrange("p t (h d) -> p t h d", h=SLAB_HEADS)
+                    if first_tile == 0:
+                        nc.scalar.copy(out=result_by_tile, in_=sums_by_head)
+                    else:
+                        nc.vector.tensor_copy(out=result_by_tile, in_=sums_by_head)
+                nc.sync.dma_start(
+                    out=slab_rows[s][:, :, first_tile : first_tile + 2, :], in_=result[:]
+                )

@@ -30,6 +30,7 @@ X_SLABS = POSITIONS // SLAB
 W_SLABS = (Q_HEADS + K_HEADS + V_HEADS) // SLAB_HEADS
 ROTATED_SLABS = (Q_HEADS + K_HEADS) // SLAB_HEADS
 RAW_SLABS_IN_SBUF = 8
+SORTED_AHEAD = 2
 
 FLOPS = 2 * POSITIONS * K * (Q_HEADS + K_HEADS + V_HEADS) * HEAD
 
@@ -49,6 +50,7 @@ def tile_rlaattention_pa_kernel(tc, x, freqs_cis, Wqkv, out_0, out_1, out_2):
         ctx.enter_context(tc.manual_schedule())
         keep = ctx.enter_context(tc.tile_pool(name="keep", bufs=1))
         raw_pool = ctx.enter_context(tc.tile_pool(name="raw", bufs=RAW_SLABS_IN_SBUF))
+        sorting = ctx.enter_context(tc.tile_pool(name="sorting", bufs=3))
         stage = ctx.enter_context(tc.tile_pool(name="stage", bufs=2 * PASSES))
         w_mx = ctx.enter_context(tc.tile_pool(name="w_mx", bufs=3))
         products = ctx.enter_context(tc.tile_pool(name="products", bufs=4))
@@ -64,14 +66,29 @@ def tile_rlaattention_pa_kernel(tc, x, freqs_cis, Wqkv, out_0, out_1, out_2):
             )
             return w_raw
 
-        def quantise_slab(raw, codes, scales, vector_helps):
+        def sort_w_slab(s):
+            w_sorted = sorting.tile([P, SLAB_TILES, PASSES, 2, P], F32, tag="w_sorted")
+            for r, copy in ((0, nc.scalar.copy), (1, nc.vector.tensor_copy)):
+                copy(
+                    out=w_sorted[:, r],
+                    in_=w_raws[s][:, r, :]
+                    .bitcast(F32)
+                    .rearrange("p (c m u) -> p c u m", c=PASSES, u=2),
+                )
+            return w_sorted
+
+        def every_2nd_word(raw):
+            words = raw[:].bitcast(F32)
+            return lambda r, c, u: words[:, r, WORDS * c + u : WORDS * (c + 1) : 2]
+
+        def quantise_slab(words, codes, scales, vector_helps):
             for c in range(PASSES):
                 flipped = flipped_banks.tile([P, 2, SLAB], F32, tag="flipped")
                 for u in range(2):
                     for r in range(SLAB_TILES):
                         nc.tensor.transpose(
                             flipped[:, u, P * r : P * (r + 1)],
-                            raw[:, r, :].bitcast(F32)[:, WORDS * c + u : WORDS * (c + 1) : 2],
+                            words(r, c, u),
                             identity[:],
                         )
                 grouped = stage.tile([P, 4 * SLAB], BF16, tag="grouped", align_bytes=64)
@@ -112,16 +129,29 @@ def tile_rlaattention_pa_kernel(tc, x, freqs_cis, Wqkv, out_0, out_1, out_2):
         x_scales = keep.tile([P, PASSES, POSITIONS], U8, align_bytes=64)
         for s in range(X_SLABS):
             columns = slice(SLAB * s, SLAB * (s + 1))
-            quantise_slab(x_raws[s], x_codes[:, :, columns], x_scales[:, :, columns], True)
+            quantise_slab(
+                every_2nd_word(x_raws[s]),
+                x_codes[:, :, columns],
+                x_scales[:, :, columns],
+                True,
+            )
 
         def prepare_w_slab(s):
             w_codes = w_mx.tile([P, PASSES, SLAB], U32, tag="w_codes", align_bytes=64)
             w_scales = w_mx.tile([P, PASSES, SLAB], U8, tag="w_scales", align_bytes=64)
-            quantise_slab(w_raws[s], w_codes, w_scales, s <= 1)
+            if s < SORTED_AHEAD:
+                words = every_2nd_word(w_raws[s])
+            else:
+                w_sorted = w_sorteds[s - SORTED_AHEAD]
+                words = lambda r, c, u: w_sorted[:, r, c, u, :]
+            quantise_slab(words, w_codes, w_scales, s <= 1)
+            if s + SORTED_AHEAD < W_SLABS:
+                w_sorteds.append(sort_w_slab(s + SORTED_AHEAD))
             if s + RAW_SLABS_IN_SBUF < W_SLABS:
                 w_raws.append(load_w_slab(s + RAW_SLABS_IN_SBUF))
             return w_codes, w_scales
 
+        w_sorteds = []
         by_member = [P, 2, SLAB_HEADS, PAIRS, 2]
         prepared = prepare_w_slab(0)
         for s in range(W_SLABS):

@@ -67,14 +67,13 @@ def tile_rlaattention_pa_kernel(tc, x, freqs_cis, Wqkv, out_0, out_1, out_2):
             return w_raw
 
         def sort_w_slab(s):
-            w_sorted = sorting.tile([P, SLAB_TILES, PASSES, 2, P], F32, tag="w_sorted")
-            for r, copy in ((0, nc.scalar.copy), (1, nc.vector.tensor_copy)):
-                copy(
-                    out=w_sorted[:, r],
-                    in_=w_raws[s][:, r, :]
-                    .bitcast(F32)
-                    .rearrange("p (c m u) -> p c u m", c=PASSES, u=2),
-                )
+            w_sorted = sorting.tile([P, PASSES, 2, P], F32, tag="w_sorted")
+            nc.scalar.copy(
+                out=w_sorted[:],
+                in_=w_raws[s][:, 0, :]
+                .bitcast(F32)
+                .rearrange("p (c m u) -> p c u m", c=PASSES, u=2),
+            )
             return w_sorted
 
         def every_2nd_word(raw):
@@ -139,11 +138,12 @@ def tile_rlaattention_pa_kernel(tc, x, freqs_cis, Wqkv, out_0, out_1, out_2):
         def prepare_w_slab(s):
             w_codes = w_mx.tile([P, PASSES, SLAB], U32, tag="w_codes", align_bytes=64)
             w_scales = w_mx.tile([P, PASSES, SLAB], U8, tag="w_scales", align_bytes=64)
+            unsorted = every_2nd_word(w_raws[s])
             if s < SORTED_AHEAD:
-                words = every_2nd_word(w_raws[s])
+                words = unsorted
             else:
                 w_sorted = w_sorteds[s - SORTED_AHEAD]
-                words = lambda r, c, u: w_sorted[:, r, c, u, :]
+                words = lambda r, c, u: unsorted(r, c, u) if r else w_sorted[:, c, u, :]
             quantise_slab(words, w_codes, w_scales, s <= 1)
             if s + SORTED_AHEAD < W_SLABS:
                 w_sorteds.append(sort_w_slab(s + SORTED_AHEAD))

@@ -59,7 +59,7 @@ def tile_rlaattention_pa_kernel(tc, x, freqs_cis, Wqkv, out_0, out_1, out_2):
         sum_banks = ctx.enter_context(tc.psum_pool(name="sum_banks", bufs=4))
 
         def load_w_slab(s):
-            w_raw = raw_pool.tile([P, SLAB_TILES, K], BF16, tag="w_raw")
+            w_raw = raw_pool.tile([P, SLAB_TILES, K], BF16, tag="w_raw", align_bytes=256)
             nc.sync.dma_start(
                 out=w_raw[:],
                 in_=Wqkv[SLAB * s : SLAB * (s + 1), :].rearrange("(r p) k -> p r k", p=P),
@@ -67,7 +67,7 @@ def tile_rlaattention_pa_kernel(tc, x, freqs_cis, Wqkv, out_0, out_1, out_2):
             return w_raw
 
         def sort_w_slab(s):
-            w_sorted = sorting.tile([P, PASSES, 2, P], F32, tag="w_sorted")
+            w_sorted = sorting.tile([P, PASSES, 2, P], F32, tag="w_sorted", align_bytes=256)
             nc.scalar.copy(
                 out=w_sorted[:],
                 in_=w_raws[s][:, 0, :]
@@ -88,7 +88,7 @@ def tile_rlaattention_pa_kernel(tc, x, freqs_cis, Wqkv, out_0, out_1, out_2):
                         nc.tensor.transpose(
                             flipped[:, u, P * r : P * (r + 1)],
                             words(r, c, u),
-                            identity[:],
+                            identity,
                         )
                 grouped = stage.tile([P, 4 * SLAB], BF16, tag="grouped", align_bytes=64)
                 side_by_side = grouped[:].bitcast(F32).rearrange("p (n u) -> p n u", u=2)
@@ -107,15 +107,16 @@ def tile_rlaattention_pa_kernel(tc, x, freqs_cis, Wqkv, out_0, out_1, out_2):
         )
         x_raws = []
         for s in range(X_SLABS):
-            x_raw = keep.tile([P, SLAB_TILES, K], BF16, name="x_raw%d" % s)
+            x_raw = keep.tile([P, SLAB_TILES, K], BF16, name="x_raw%d" % s, align_bytes=256)
             nc.sync.dma_start(
                 out=x_raw[:], in_=x_rows[:, SLAB_TILES * s : SLAB_TILES * (s + 1), :]
             )
             x_raws.append(x_raw)
         w_raws = [load_w_slab(s) for s in range(RAW_SLABS_IN_SBUF)]
 
-        identity = keep.tile([P, P], F32)
-        make_identity(nc, identity[:])
+        identity_room = keep.tile([P, P + 32], F32, align_bytes=256)
+        identity = identity_room[:, 32:]
+        make_identity(nc, identity)
 
         for_even = keep.tile([P, TILES, PAIRS, 2], F32)
         for_odd = keep.tile([P, TILES, PAIRS, 2], F32)
@@ -124,8 +125,9 @@ def tile_rlaattention_pa_kernel(tc, x, freqs_cis, Wqkv, out_0, out_1, out_2):
         nc.vector.tensor_scalar_mul(for_odd[:, :, :, 0], freq_raw[:, :, :, 0], -1.0)
         nc.vector.tensor_copy(out=for_odd[:, :, :, 1], in_=freq_raw[:, :, :, 1])
 
-        x_codes = keep.tile([P, PASSES, POSITIONS], U32, align_bytes=64)
-        x_scales = keep.tile([P, PASSES, POSITIONS], U8, align_bytes=64)
+        x_codes = keep.tile([P, PASSES, POSITIONS], U32, align_bytes=256)
+        x_scales_room = keep.tile([P, 64 + PASSES * POSITIONS], U8, align_bytes=256)
+        x_scales = x_scales_room[:, 64:].rearrange("p (c n) -> p c n", c=PASSES)
         for s in range(X_SLABS):
             columns = slice(SLAB * s, SLAB * (s + 1))
             quantise_slab(
@@ -136,8 +138,10 @@ def tile_rlaattention_pa_kernel(tc, x, freqs_cis, Wqkv, out_0, out_1, out_2):
             )
 
         def prepare_w_slab(s):
-            w_codes = w_mx.tile([P, PASSES, SLAB], U32, tag="w_codes", align_bytes=64)
-            w_scales = w_mx.tile([P, PASSES, SLAB], U8, tag="w_scales", align_bytes=64)
+            codes_room = w_mx.tile([P, 32 + PASSES * SLAB], U32, tag="w_codes", align_bytes=256)
+            scales_room = w_mx.tile([P, 192 + PASSES * SLAB], U8, tag="w_scales", align_bytes=256)
+            w_codes = codes_room[:, 32:].rearrange("p (c n) -> p c n", c=PASSES)
+            w_scales = scales_room[:, 192:].rearrange("p (c n) -> p c n", c=PASSES)
             unsorted = every_2nd_word(w_raws[s])
             if s < SORTED_AHEAD:
                 words = unsorted

from contextlib import ExitStack

import concourse.mybir as mybir
from concourse.masks import make_identity

F32 = mybir.dt.float32
BF16 = mybir.dt.bfloat16
U32 = mybir.dt.uint32
U8 = mybir.dt.uint8
FP8X4 = mybir.dt.float8_e4m3fn_x4
MULT = mybir.AluOpType.mult
ADD = mybir.AluOpType.add

P = 128
POSITIONS = 512
K = 2048
HEAD = 128
PAIRS = HEAD // 2
Q_HEADS, K_HEADS, V_HEADS = 16, 4, 4

K_PASS = 4 * P
PASSES = K // K_PASS
WORDS = K_PASS // 2

SLAB = 256
SLAB_TILES = SLAB // P
SLAB_HEADS = SLAB // HEAD
TILES = POSITIONS // P
X_SLABS = POSITIONS // SLAB
W_SLABS = (Q_HEADS + K_HEADS + V_HEADS) // SLAB_HEADS
ROTATED_SLABS = (Q_HEADS + K_HEADS) // SLAB_HEADS
RAW_SLABS_IN_SBUF = 8
SORTED_AHEAD = 2

FLOPS = 2 * POSITIONS * K * (Q_HEADS + K_HEADS + V_HEADS) * HEAD


def tile_rlaattention_pa_kernel(tc, x, freqs_cis, Wqkv, out_0, out_1, out_2):
    nc = tc.nc

    x_rows = x.flatten_outer_dims().rearrange("(p i) k -> p i k", i=TILES)
    freq_rows = freqs_cis.rearrange("(p i) d -> p i d", i=TILES)
    slab_rows = [
        out.rearrange("b h (p i) d -> p (b h) i d", i=TILES)[:, h : h + SLAB_HEADS]
        for out, heads in ((out_0, Q_HEADS), (out_1, K_HEADS), (out_2, V_HEADS))
        for h in range(0, heads, SLAB_HEADS)
    ]

    with ExitStack() as ctx:
        ctx.enter_context(tc.manual_schedule())
        keep = ctx.enter_context(tc.tile_pool(name="keep", bufs=1))
        raw_pool = ctx.enter_context(tc.tile_pool(name="raw", bufs=RAW_SLABS_IN_SBUF))
        sorting = ctx.enter_context(tc.tile_pool(name="sorting", bufs=3))
        stage = ctx.enter_context(tc.tile_pool(name="stage", bufs=2 * PASSES))
        w_mx = ctx.enter_context(tc.tile_pool(name="w_mx", bufs=3))
        products = ctx.enter_context(tc.tile_pool(name="products", bufs=4))
        results = ctx.enter_context(tc.tile_pool(name="results", bufs=10))
        flipped_banks = ctx.enter_context(tc.psum_pool(name="flipped_banks", bufs=4))
        sum_banks = ctx.enter_context(tc.psum_pool(name="sum_banks", bufs=4))

        def load_w_slab(s):
            w_raw = raw_pool.tile([P, SLAB_TILES, K], BF16, tag="w_raw", align_bytes=256)
            nc.sync.dma_start(
                out=w_raw[:],
                in_=Wqkv[SLAB * s : SLAB * (s + 1), :].rearrange("(r p) k -> p r k", p=P),
            )
            return w_raw

        def sort_w_slab(s):
            w_sorted = sorting.tile([P, PASSES, 2, P], F32, tag="w_sorted", align_bytes=256)
            nc.scalar.copy(
                out=w_sorted[:],
                in_=w_raws[s][:, 0, :]
                .bitcast(F32)
                .rearrange("p (c m u) -> p c u m", c=PASSES, u=2),
            )
            return w_sorted

        def every_2nd_word(raw):
            words = raw[:].bitcast(F32)
            return lambda r, c, u: words[:, r, WORDS * c + u : WORDS * (c + 1) : 2]

        def quantise_slab(words, codes, scales, vector_helps):
            for c in range(PASSES):
                flipped = flipped_banks.tile([P, 2, SLAB], F32, tag="flipped")
                for u in range(2):
                    for r in range(SLAB_TILES):
                        nc.tensor.transpose(
                            flipped[:, u, P * r : P * (r + 1)],
                            words(r, c, u),
                            identity,
                        )
                grouped = stage.tile([P, 4 * SLAB], BF16, tag="grouped", align_bytes=64)
                side_by_side = grouped[:].bitcast(F32).rearrange("p (n u) -> p n u", u=2)
                planes = flipped[:].rearrange("p u n -> p n u")
                if vector_helps and c == 1:
                    nc.vector.tensor_copy(out=side_by_side, in_=planes)
                else:
                    nc.scalar.copy(out=side_by_side, in_=planes)
                nc.vector.quantize_mx(
                    out=codes[:, c, :].bitcast(FP8X4), scales=scales[:, c, :], in_=grouped[:]
                )

        freq_raw = keep.tile([P, TILES, PAIRS, 2], BF16)
        nc.scalar.dma_start(
            out=freq_raw[:].rearrange("p i j e -> p i (j e)"), in_=freq_rows
        )
        x_raws = []
        for s in range(X_SLABS):
            x_raw = keep.tile([P, SLAB_TILES, K], BF16, name="x_raw%d" % s, align_bytes=256)
            nc.sync.dma_start(
                out=x_raw[:], in_=x_rows[:, SLAB_TILES * s : SLAB_TILES * (s + 1), :]
            )
            x_raws.append(x_raw)
        w_raws = [load_w_slab(s) for s in range(RAW_SLABS_IN_SBUF)]

        identity_room = keep.tile([P, P + 32], F32, align_bytes=256)
        identity = identity_room[:, 32:]
        make_identity(nc, identity)

        for_even = keep.tile([P, TILES, PAIRS, 2], F32)
        for_odd = keep.tile([P, TILES, PAIRS, 2], F32)
        nc.vector.tensor_copy(out=for_even[:, :, :, 0], in_=freq_raw[:, :, :, 1])
        nc.vector.tensor_copy(out=for_even[:, :, :, 1], in_=freq_raw[:, :, :, 0])
        nc.vector.tensor_scalar_mul(for_odd[:, :, :, 0], freq_raw[:, :, :, 0], -1.0)
        nc.vector.tensor_copy(out=for_odd[:, :, :, 1], in_=freq_raw[:, :, :, 1])

        x_codes = keep.tile([P, PASSES, POSITIONS], U32, align_bytes=256)
        x_scales_room = keep.tile([P, 64 + PASSES * POSITIONS], U8, align_bytes=256)
        x_scales = x_scales_room[:, 64:].rearrange("p (c n) -> p c n", c=PASSES)
        for s in range(X_SLABS):
            columns = slice(SLAB * s, SLAB * (s + 1))
            quantise_slab(
                every_2nd_word(x_raws[s]),
                x_codes[:, :, columns],
                x_scales[:, :, columns],
                True,
            )

        def prepare_w_slab(s):
            codes_room = w_mx.tile([P, 32 + PASSES * SLAB], U32, tag="w_codes", align_bytes=256)
            scales_room = w_mx.tile([P, 192 + PASSES * SLAB], U8, tag="w_scales", align_bytes=256)
            w_codes = codes_room[:, 32:].rearrange("p (c n) -> p c n", c=PASSES)
            w_scales = scales_room[:, 192:].rearrange("p (c n) -> p c n", c=PASSES)
            unsorted = every_2nd_word(w_raws[s])
            if s < SORTED_AHEAD:
                words = unsorted
            else:
                w_sorted = w_sorteds[s - SORTED_AHEAD]
                words = lambda r, c, u: unsorted(r, c, u) if r else w_sorted[:, c, u, :]
            quantise_slab(words, w_codes, w_scales, s <= 1)
            if s + SORTED_AHEAD < W_SLABS:
                w_sorteds.append(sort_w_slab(s + SORTED_AHEAD))
            if s + RAW_SLABS_IN_SBUF < W_SLABS:
                w_raws.append(load_w_slab(s + RAW_SLABS_IN_SBUF))
            return w_codes, w_scales

        w_sorteds = []
        by_member = [P, 2, SLAB_HEADS, PAIRS, 2]
        prepared = prepare_w_slab(0)
        for s in range(W_SLABS):
            w_codes, w_scales = prepared
            if s + 1 < W_SLABS:
                prepared = prepare_w_slab(s + 1)

            for first_tile in range(0, TILES, 2):
                sums = sum_banks.tile([P, 2, SLAB], F32, tag="sums")
                for t in range(2):
                    positions = slice(P * (first_tile + t), P * (first_tile + t + 1))
                    for c in range(PASSES):
                        nc.tensor.matmul_mx(
                            out=sums[:, t, :],
                            lhsT=x_codes[:, c, positions].bitcast(FP8X4),
                            lhsT_scale=x_scales[:, c, positions],
                            rhs=w_codes[:, c, :].bitcast(FP8X4),
                            rhs_scale=w_scales[:, c, :],
                            start=(c == 0),
                            stop=(c == PASSES - 1),
                        )
                result = results.tile([P, SLAB_HEADS, 2, HEAD], F32, tag="result")
                result_by_tile = result[:].rearrange("p h t d -> p t h d")
                if s < ROTATED_SLABS:
                    members = sums[:].rearrange(
                        "p t (h j e) -> p t h j e", h=SLAB_HEADS, e=2
                    )
                    tiles = slice(first_tile, first_tile + 2)
                    from_even = products.tile(by_member, F32, tag="from_even")
                    from_odd = products.tile(by_member, F32, tag="from_odd")
                    nc.vector.tensor_tensor(
                        out=from_even[:],
                        in0=members[:, :, :, :, 0:1].to_broadcast(by_member),
                        in1=for_even[:, tiles].unsqueeze(2).to_broadcast(by_member),
                        op=MULT,
                    )
                    nc.vector.tensor_tensor(
                        out=from_odd[:],
                        in0=members[:, :, :, :, 1:2].to_broadcast(by_member),
                        in1=for_odd[:, tiles].unsqueeze(2).to_broadcast(by_member),
                        op=MULT,
                    )
                    nc.gpsimd.tensor_tensor(
                        out=result_by_tile,
                        in0=from_even[:].rearrange("p t h j e -> p t h (j e)"),
                        in1=from_odd[:].rearrange("p t h j e -> p t h (j e)"),
                        op=ADD,
                    )
                else:
                    sums_by_head = sums[:].rearrange("p t (h d) -> p t h d", h=SLAB_HEADS)
                    if first_tile == 0:
                        nc.scalar.copy(out=result_by_tile, in_=sums_by_head)
                    else:
                        nc.vector.tensor_copy(out=result_by_tile, in_=sums_by_head)
                nc.sync.dma_start(
                    out=slab_rows[s][:, :, first_tile : first_tile + 2, :], in_=result[:]
                )
